import numpy as np
import ml_dtypes


def mxq(x, axis, fmt="e4m3"):
    dtype, down = {"e4m3": (ml_dtypes.float8_e4m3fn, 7), "e5m2": (ml_dtypes.float8_e5m2, 14)}[fmt]
    v = np.moveaxis(np.asarray(x, np.float32).astype(ml_dtypes.bfloat16).astype(np.float64), axis, -1)
    blocks = v.reshape(v.shape[:-1] + (-1, 32))
    amax = np.abs(blocks).max(-1, keepdims=True)
    byte = np.maximum(np.where(amax > 0, np.frexp(amax)[1] - 1 + 127, 0) - down, 1)
    scale = np.exp2(byte - 127.0)
    codes = (blocks / scale).astype(np.float32).astype(dtype).astype(np.float64)
    return np.moveaxis((codes * scale).reshape(v.shape), -1, axis)


WIDE = False


def mx_kscale(k):
    if not WIDE:
        return np.ones(k)
    levels = np.array([18, -18])
    if k % 512:
        return np.exp2(np.random.permutation(np.resize(levels, k // 32))).repeat(32)
    a = np.empty((k // 512, 16))
    for p in range(k // 512):
        a[p, :8] = np.random.permutation(np.resize(levels, 8))
        for g in range(8):
            far = levels[np.abs(levels - a[p, g]) >= 10]
            a[p, g + 8] = far[np.random.randint(len(far))]
    return np.exp2(a.ravel()).repeat(32)


BF16 = ml_dtypes.bfloat16


def bf(x):
    return np.asarray(x, np.float32).astype(BF16)


def f64(x):
    return np.asarray(x).astype(np.float64)


B, IN_DIM, R_IN, R_OUT = 1024, 1024, 1024, 1024
HIDDEN = R_IN + R_OUT
BASELINE_THRE = 0.1
BETA = 1.8
R_M = 3.0
DT = 1.0


def sigmoid(v):
    return 1.0 / (1.0 + np.exp(-v))


def setup_inputs():
    s = mx_kscale(B)[:, None]
    u = mx_kscale(R_IN)
    return {
        "x_t": bf(np.random.standard_normal((B, IN_DIM)) * s),
        "spk_t": bf(np.random.random((B, HIDDEN)) < 0.3),
        "mem_t_in": bf(np.random.standard_normal((B, R_IN))),
        "b_t_in": bf(np.random.random((B, R_IN))),
        "W_x2in": bf(np.random.standard_normal((R_IN, IN_DIM)) / np.sqrt(IN_DIM) / u[:, None]),
        "b_x2in": bf(np.random.standard_normal(R_IN) * 0.5),
        "W_rec4in": bf(np.random.standard_normal((R_IN, R_IN)) * 1.5 / np.sqrt(R_IN)),
        "b_rec4in": bf(np.random.standard_normal(R_IN) * 0.5),
        "W_out2in": bf(np.random.standard_normal((R_IN, R_OUT)) * 1.5 / np.sqrt(R_OUT)),
        "b_out2in": bf(np.random.standard_normal(R_IN) * 0.5),
        "tau_adp_in": bf(1.5 + 0.5 * np.random.standard_normal(R_IN)),
        "tau_m_in": bf(2.0 + 0.5 * np.random.standard_normal(R_IN)),
        "grad_out": bf(4.0 * np.random.standard_normal((B, R_IN)) * np.exp2(np.random.randint(-6, 1, (B, 1))) / s * u),
    }


def reference(x_t, spk_t, mem_t_in, b_t_in, W_x2in, b_x2in, W_rec4in, b_rec4in, W_out2in, b_out2in, tau_adp_in, tau_m_in, grad_out):
    a = sigmoid(f64(tau_m_in))
    dr = f64(grad_out) * ((1.0 - a) * R_M)
    dx = mxq(dr, 1, "e5m2") @ mxq(f64(W_x2in), 1 - 1, "e4m3")
    dw = mxq(dr, 0, "e5m2").T @ mxq(f64(x_t), 0, "e4m3")
    return dx, dw

from contextlib import ExitStack

import concourse.mybir as mybir
from concourse.masks import make_identity

B, IN_DIM, R_IN = 1024, 1024, 1024
R_M = 3.0
FLOPS = 2 * 2 * B * IN_DIM * R_IN
BYTES = 2 * (B * IN_DIM + R_IN * IN_DIM + B * R_IN + R_IN) + 4 * (B * IN_DIM + R_IN * IN_DIM)

F32 = mybir.dt.float32
BF16 = mybir.dt.bfloat16
U32 = mybir.dt.uint32
U8 = mybir.dt.uint8
E4M3 = mybir.dt.float8_e4m3fn_x4
E5M2 = mybir.dt.float8_e5m2_x4
ACT = mybir.ActivationFunctionType
ALU = mybir.AluOpType

P = 128
PACK = 4
K_PASS = 512
N_TILE = 512
RUN = 4


def tile_snnlayer_pa_v_kernel(
    tc, x_t, spk_t, mem_t_in, b_t_in, W_x2in, b_x2in, W_rec4in, b_rec4in, W_out2in, b_out2in,
    tau_adp_in, tau_m_in, grad_out, out_0, out_1,
):
    nc = tc.nc
    V, S = nc.vector, nc.scalar

    with ExitStack() as ctx:
        keep = ctx.enter_context(tc.tile_pool(name="keep", bufs=1))
        stage = ctx.enter_context(tc.tile_pool(name="stage", bufs=4))
        results = ctx.enter_context(tc.tile_pool(name="results", bufs=8))
        psum = ctx.enter_context(tc.psum_pool(name="psum", bufs=8))
        ctx.enter_context(tc.manual_schedule())

        def kept(name, shape, dtype):
            return keep.tile(shape, dtype, name=name, align_bytes=64)

        def copy(eng, out, in_):
            if eng is V:
                nc.vector.tensor_copy(out=out, in_=in_)
            else:
                nc.scalar.copy(out=out, in_=in_)

        g_rows = grad_out.rearrange("(h m pair e) r -> h pair m e r", h=2, pair=2, e=2)
        x_rows = x_t.rearrange("(h p t) i -> h p t i", h=2, t=PACK)
        w_rows = W_x2in.rearrange("(g p t) i -> g p t i", g=2, t=PACK)
        dx_rows = out_0.rearrange("(h m pair e) i -> h pair e m i", h=2, pair=2, e=2)
        dw_rows = out_1.rearrange("(g p t) i -> g t p i", g=2, t=PACK)

        tau = kept("tau", [P, 2, PACK], BF16)
        nc.scalar.dma_start(out=tau[:], in_=tau_m_in.rearrange("(g p t) -> p g t", g=2, t=PACK))

        g_raw, x_raw, w_raw = {}, {}, {}

        def load_g(h, pair):
            g_raw[h, pair] = kept("g_raw%d%d" % (h, pair), [P, 2, R_IN], BF16)
            nc.sync.dma_start(out=g_raw[h, pair][:], in_=g_rows[h, pair])

        def load_rows(raw, rows, name, k):
            raw[k] = kept("%s_raw%d" % (name, k), [P, PACK, IN_DIM], BF16)
            nc.sync.dma_start(out=raw[k][:], in_=rows[k])

        load_g(0, 0)
        load_rows(w_raw, w_rows, "w", 0)
        load_g(0, 1)
        load_rows(w_raw, w_rows, "w", 1)
        load_g(1, 0)
        load_g(1, 1)
        load_rows(x_raw, x_rows, "x", 0)
        load_rows(x_raw, x_rows, "x", 1)

        ident = kept("ident", [P, P], F32)
        make_identity(nc, ident[:])

        leak = kept("leak", [P, 2 * PACK], F32)
        gain = kept("gain", [P, 2 * PACK], F32)
        nc.scalar.activation(out=leak[:], in_=tau[:].rearrange("p g t -> p (g t)"), func=ACT.Sigmoid, scale=-1.0)
        nc.scalar.activation(out=gain[:], in_=leak[:], func=ACT.Copy, scale=R_M)

        banks = {}
        drT = {}
        grouped = {}
        codes, scales = {}, {}

        def turn_g(h, pair, g):
            bank = psum.tile([P, 2, 2, P], F32, name="bank")
            words = g_raw[h, pair][:].rearrange("m e r -> m (e r)").bitcast(F32)
            for u in range(2):
                for e in range(2):
                    first = e * 512 + g * 256 + u
                    nc.tensor.transpose(bank[:, u, e, :], words[:, first : first - u + 256 : 2], ident[:])
            banks["g", h, pair, g] = bank

        def scale_g(eng, h, pair, g):
            bank = banks["g", h, pair, g]
            halves = bank[:].rearrange("p u e m -> p (u e m)").bitcast(BF16)
            halves = halves.rearrange("p (u e m lo) -> p u lo m e", u=2, e=2, lo=2)
            dr = kept("drT%d%d%d" % (h, pair, g), [P, PACK, 2 * P], BF16)
            drT[h, pair, g] = dr
            for t in range(PACK):
                out = dr[:, t, :].rearrange("p (m e) -> p m e", e=2)
                in_ = halves[:, t // 2, t % 2, :, :]
                col = gain[:, PACK * g + t : PACK * g + t + 1]
                if eng is V:
                    nc.vector.tensor_scalar(out=out, in0=in_, scalar1=col, scalar2=None, op0=ALU.mult)
                else:
                    nc.scalar.activation(out=out, in_=in_, func=ACT.Copy, scale=col)

        def group_rows(eng, name, raw, k, n):
            tile = stage.tile([P, PACK * N_TILE], BF16, name="grouped", align_bytes=64)
            src = raw[k][:, :, n * N_TILE : (n + 1) * N_TILE]
            copy(
                eng,
                tile[:].rearrange("p (c i t) -> p c t i", i=RUN, t=PACK),
                src.rearrange("p t (c i) -> p c t i", i=RUN),
            )
            grouped[name, k, n] = tile

        def group_dr(h, pair):
            tile = stage.tile([P, PACK * N_TILE], BF16, name="grouped", align_bytes=64)
            for g in range(2):
                dst = tile[:, g * 1024 : (g + 1) * 1024]
                nc.vector.tensor_copy(
                    out=dst.rearrange("p (e c i t) -> p e c t i", e=2, i=RUN, t=PACK),
                    in_=drT[h, pair, g][:].rearrange("p t (c i e) -> p e c t i", i=RUN, e=2),
                )
            grouped["f", h, pair] = tile

        def turn_dr(g, t):
            bank = psum.tile([P, 2, 2, P], F32, name="bank")
            for h in range(2):
                for pair in range(2):
                    nc.tensor.transpose(bank[:, h, pair, :], drT[h, pair, g][:, t, :].bitcast(F32), ident[:])
            banks["t", g, t] = bank

        def group_turned(eng, g, t):
            tile = stage.tile([P, 2 * N_TILE], BF16, name="turned", align_bytes=64)
            copy(
                eng,
                tile[:].bitcast(F32).rearrange("q (h p pair) -> q h p pair", h=2, pair=2),
                banks["t", g, t][:].rearrange("q h pair p -> q h p pair"),
            )
            grouped["t", g, t] = tile

        def quantise(key):
            tile = grouped[key]
            width = tile.shape[1] // PACK
            label = "%s%d%d" % key
            codes[key] = kept("codes_" + label, [P, width], U32)
            scales[key] = kept("scales_" + label, [P, width], U8)
            fmt = E4M3 if key[0] in "xw" else E5M2
            nc.vector.quantize_mx(out=codes[key][:].bitcast(fmt), scales=scales[key][:], in_=tile[:])

        def product(key, lhs, cols, rhs_name, n):
            bank = psum.tile([P, N_TILE], F32, name="bank")
            for k in range(2):
                nc.tensor.matmul_mx(
                    out=bank[:],
                    lhsT=codes[lhs][:, cols[k]].bitcast(E5M2),
                    lhsT_scale=scales[lhs][:, cols[k]],
                    rhs=codes[rhs_name, k, n][:].bitcast(E4M3),
                    rhs_scale=scales[rhs_name, k, n][:],
                    start=(k == 0),
                    stop=(k == 1),
                )
            banks[key] = bank

        def dx_product(h, pair, e, n):
            cols = [slice(256 * g + P * e, 256 * g + P * (e + 1)) for g in range(2)]
            product(("dx", h, pair, e, n), ("f", h, pair), cols, "w", n)

        def dw_product(g, t, n):
            cols = [slice(P * h, P * (h + 1)) for h in range(2)]
            product(("dw", g, t, n), ("t", g, t), cols, "x", n)

        def store(key, rows, engines, halves=(0, 1)):
            res = results.tile([P, IN_DIM], F32, name="res")
            for n, eng in zip(halves, engines):
                copy(eng, res[:, n * N_TILE : (n + 1) * N_TILE], banks[key + (n,)][:])
            cols = slice(halves[0] * N_TILE, (halves[-1] + 1) * N_TILE)
            nc.sync.dma_start(out=rows[:, cols], in_=res[:, cols])

        def dx_pair(h, pair, e):
            dx_product(h, pair, e, 0)
            dx_product(h, pair, e, 1)

        def dw_pair(g, t):
            dw_product(g, t, 0)
            dw_product(g, t, 1)

        def dx_store(h, pair, e, engines=(S, S)):
            store(("dx", h, pair, e), dx_rows[h, pair, e], engines)

        def dw_store(g, t, engines=(S, S), halves=(0, 1)):
            store(("dw", g, t), dw_rows[g, t], engines, halves)

        turn_g(0, 0, 0)
        turn_g(0, 0, 1)
        scale_g(S, 0, 0, 0)
        scale_g(V, 0, 0, 1)
        group_rows(S, "w", w_raw, 0, 1)
        group_dr(0, 0)
        group_rows(V, "w", w_raw, 0, 0)
        quantise(("f", 0, 0))
        quantise(("w", 0, 0))
        quantise(("w", 0, 1))
        turn_g(0, 1, 0)
        turn_g(0, 1, 1)
        scale_g(S, 0, 1, 0)
        scale_g(S, 0, 1, 1)
        group_rows(V, "w", w_raw, 1, 0)
        group_rows(V, "w", w_raw, 1, 1)
        quantise(("w", 1, 0))
        quantise(("w", 1, 1))
        for pair in range(2):
            turn_g(1, pair, 0)
            turn_g(1, pair, 1)
        scale_g(S, 1, 0, 0)
        scale_g(S, 1, 0, 1)
        group_dr(0, 1)
        group_dr(1, 0)
        quantise(("f", 0, 1))
        quantise(("f", 1, 0))
        dx_pair(0, 0, 0)
        dx_pair(0, 0, 1)
        scale_g(S, 1, 1, 0)
        dx_store(0, 0, 0)
        scale_g(S, 1, 1, 1)
        dx_store(0, 0, 1)
        group_rows(V, "x", x_raw, 0, 0)
        group_dr(1, 1)
        quantise(("x", 0, 0))
        quantise(("f", 1, 1))
        dx_pair(0, 1, 0)
        dx_pair(0, 1, 1)
        dx_store(0, 1, 0)
        dx_pair(1, 0, 0)
        dx_store(0, 1, 1)
        dx_pair(1, 0, 1)
        dx_store(1, 0, 0)
        turn_dr(0, 0)
        turn_dr(0, 1)
        dx_store(1, 0, 1)
        group_turned(S, 0, 0)
        group_turned(S, 0, 1)
        group_rows(V, "x", x_raw, 1, 0)
        group_rows(V, "x", x_raw, 0, 1)
        quantise(("x", 1, 0))
        quantise(("t", 0, 0))
        quantise(("t", 0, 1))
        dx_pair(1, 1, 0)
        turn_dr(0, 2)
        turn_dr(0, 3)
        dx_store(1, 1, 0)
        dx_pair(1, 1, 1)
        group_turned(S, 0, 2)
        group_turned(S, 0, 3)
        group_rows(V, "x", x_raw, 1, 1)
        quantise(("t", 0, 2))
        quantise(("t", 0, 3))
        quantise(("x", 0, 1))
        quantise(("x", 1, 1))
        dx_store(1, 1, 1)
        for t in range(4):
            dw_product(0, t, 0)
        for t in range(4):
            turn_dr(1, t)
        for t in range(4):
            dw_store(0, t, (S,), (0,))
        for t in range(4):
            group_turned(V, 1, t)
        for t in range(4):
            quantise(("t", 1, t))
        for t in range(4):
            dw_product(0, t, 1)
        for t in range(4):
            dw_store(0, t, (S,), (1,))
        for t in range(4):
            dw_pair(1, t)
        for t in range(4):
            dw_store(1, t, (V, S))
